import numpy as np
import ml_dtypes


def mxq(x, axis, fmt="e4m3"):
    dtype, down = {"e4m3": (ml_dtypes.float8_e4m3fn, 7), "e5m2": (ml_dtypes.float8_e5m2, 14)}[fmt]
    v = np.moveaxis(np.asarray(x, np.float32).astype(ml_dtypes.bfloat16).astype(np.float64), axis, -1)
    blocks = v.reshape(v.shape[:-1] + (-1, 32))
    amax = np.abs(blocks).max(-1, keepdims=True)
    byte = np.maximum(np.where(amax > 0, np.frexp(amax)[1] - 1 + 127, 0) - down, 1)
    scale = np.exp2(byte - 127.0)
    codes = (blocks / scale).astype(np.float32).astype(dtype).astype(np.float64)
    return np.moveaxis((codes * scale).reshape(v.shape), -1, axis)


WIDE = False


def mx_kscale(k):
    if not WIDE:
        return np.ones(k)
    levels = np.array([10, -10, 5, -5, 0])
    a = np.random.permutation(np.resize(levels, k // 512 * 4)).reshape(k // 512, 4)
    idx = np.arange(k)
    return np.exp2(a[idx // 512, idx % 128 // 32])


BF16 = ml_dtypes.bfloat16


def bf(x):
    return np.asarray(x, np.float32).astype(BF16)


def f64(x):
    return np.asarray(x).astype(np.float64)


B, CIN, COUT, H, W = 4, 512, 256, 64, 64


def setup_inputs():
    s = mx_kscale(CIN)
    x = np.random.standard_normal((B, CIN, H, W)) * s[None, :, None, None]
    weight = np.random.uniform(-1.0, 1.0, (CIN, COUT)) * np.sqrt(3.0 / CIN) / s[:, None]
    return {"x": bf(x), "weight": bf(weight)}


def reference(x, weight):
    wq = mxq(f64(weight), 0, "e4m3")
    xq = mxq(f64(x), 1, "e4m3")
    return np.einsum("io,bihw->bohw", wq, xq, optimize=True)

@@ -1,0 +1,130 @@
+from contextlib import ExitStack
+
+import concourse.mybir as mybir
+
+BF16 = mybir.dt.bfloat16
+F32 = mybir.dt.float32
+U32 = mybir.dt.uint32
+U8 = mybir.dt.uint8
+FP8X4 = mybir.dt.float8_e4m3fn_x4
+
+BATCH, CIN, COUT, PIXELS = 4, 512, 256, 64 * 64
+P = 128
+PACK = 4
+O_TILES = COUT // P
+CHUNK = 1024
+CHUNKS_PER_IMAGE = PIXELS // CHUNK
+N_CHUNKS = BATCH * CHUNKS_PER_IMAGE
+N_TILE = 512
+VECTOR_PIXELS = 848
+RUN = 4
+
+FLOPS = 2 * BATCH * CIN * COUT * PIXELS
+
+
+def tile_simpleconvolution_t_kernel(tc, x, weight, out):
+    nc = tc.nc
+    x_rows = x.rearrange("b (p j) h w -> b p j (h w)", j=PACK)
+    w_rows = weight.rearrange("(p j) o -> p j o", j=PACK)
+    out_rows = out.rearrange("b (t o) h w -> b t o (h w)", o=P)
+
+    with ExitStack() as ctx:
+        big = ctx.enter_context(tc.tile_pool(name="big", bufs=1))
+        keep = ctx.enter_context(tc.tile_pool(name="keep", bufs=1))
+        stage = ctx.enter_context(tc.tile_pool(name="stage", bufs=3))
+        psum = ctx.enter_context(tc.psum_pool(name="psum", bufs=8))
+        ctx.enter_context(tc.manual_schedule())
+
+        w_raw = keep.tile([P, PACK, COUT], BF16, name="w_raw")
+        nc.sync.dma_start(out=w_raw[:], in_=w_rows)
+        x_slot = {0: "slot0", 1: "slot1", 2: "slot2", 3: "slot4"}
+        out_slot = {0: "slot3", 1: "slot0", 2: "slot1", 3: "slot2"}
+        x_tiles = []
+        for b in range(BATCH):
+            x_tile = big.tile([P, PACK, PIXELS], BF16, name="x_tile", tag=x_slot[b])
+            nc.sync.dma_start(out=x_tile[:], in_=x_rows[b])
+            x_tiles.append(x_tile)
+
+        w_grouped = keep.tile([P, COUT, PACK], BF16, name="w_grouped", align_bytes=64)
+        nc.vector.tensor_copy(out=w_grouped[:], in_=w_raw[:].rearrange("p j o -> p o j"))
+        w_codes = keep.tile([P, COUT], U32, name="w_codes", align_bytes=64)
+        w_scales = keep.tile([P, COUT], U8, name="w_scales", align_bytes=64)
+        nc.vector.quantize_mx(
+            out=w_codes[:].bitcast(FP8X4),
+            scales=w_scales[:],
+            in_=w_grouped[:].rearrange("p o j -> p (o j)"),
+        )
+
+        grouped_tiles = {}
+        code_tiles = {}
+        acc_tiles = {}
+        out_tiles = {}
+
+        def regroup(g):
+            b, q = divmod(g, CHUNKS_PER_IMAGE)
+            grouped = stage.tile([P, CHUNK, PACK], BF16, name="grouped", align_bytes=64)
+            for copy, lo, hi in (
+                (nc.vector.tensor_copy, 0, VECTOR_PIXELS),
+                (nc.scalar.copy, VECTOR_PIXELS, CHUNK),
+            ):
+                copy(
+                    out=grouped[:, lo:hi, :].rearrange("p (c i) j -> p c j i", i=RUN),
+                    in_=x_tiles[b][:, :, q * CHUNK + lo : q * CHUNK + hi].rearrange(
+                        "p j (c i) -> p c j i", i=RUN
+                    ),
+                )
+            grouped_tiles[g] = grouped
+
+        def quantise(g):
+            codes = stage.tile([P, CHUNK], U32, name="codes", align_bytes=64)
+            scales = stage.tile([P, CHUNK], U8, name="scales", align_bytes=64)
+            nc.vector.quantize_mx(
+                out=codes[:].bitcast(FP8X4),
+                scales=scales[:],
+                in_=grouped_tiles[g][:].rearrange("p c j -> p (c j)"),
+            )
+            code_tiles[g] = (codes, scales)
+
+        def multiply(g):
+            codes, scales = code_tiles[g]
+            for n in range(CHUNK // N_TILE):
+                cols = slice(n * N_TILE, (n + 1) * N_TILE)
+                for t in range(O_TILES):
+                    o_cols = slice(t * P, (t + 1) * P)
+                    acc = psum.tile([P, N_TILE], F32, name="acc")
+                    nc.tensor.matmul_mx(
+                        out=acc[:],
+                        lhsT=w_codes[:, o_cols].bitcast(FP8X4),
+                        lhsT_scale=w_scales[:, o_cols],
+                        rhs=codes[:, cols].bitcast(FP8X4),
+                        rhs_scale=scales[:, cols],
+                        start=True,
+                        stop=True,
+                    )
+                    acc_tiles[(g, n, t)] = acc
+
+        def evacuate(g):
+            b, q = divmod(g, CHUNKS_PER_IMAGE)
+            if q == 0:
+                out_tiles[b] = big.tile([P, O_TILES, PIXELS], F32, name="out_tile", tag=out_slot[b])
+            for n in range(CHUNK // N_TILE):
+                first = q * CHUNK + n * N_TILE
+                for t in range(O_TILES):
+                    nc.scalar.copy(
+                        out=out_tiles[b][:, t, first : first + N_TILE], in_=acc_tiles[(g, n, t)][:]
+                    )
+            pieces = 2 if b == BATCH - 1 else 1
+            per_piece = CHUNKS_PER_IMAGE // pieces
+            if (q + 1) % per_piece == 0:
+                px = slice((q + 1 - per_piece) * CHUNK, (q + 1) * CHUNK)
+                for t in range(O_TILES):
+                    nc.sync.dma_start(out=out_rows[b, t][:, px], in_=out_tiles[b][:, t, px])
+
+        for step in range(N_CHUNKS + 2):
+            if step < N_CHUNKS:
+                regroup(step)
+            if 0 <= step - 1 < N_CHUNKS:
+                quantise(step - 1)
+                multiply(step - 1)
+            if step - 2 >= 0:
+                evacuate(step - 2)

@@ -26,7 +26,7 @@ def tile_simpleconvolution_t_kernel(tc, x, weight, out):
     nc = tc.nc
     x_rows = x.rearrange("b (p j) h w -> b p j (h w)", j=PACK)
     w_rows = weight.rearrange("(p j) o -> p j o", j=PACK)
-    out_rows = out.rearrange("b (t o) h w -> b t o (h w)", o=P)
+    out_rows = out.rearrange("b (m t) h w -> b m t (h w)", t=O_TILES)
 
     with ExitStack() as ctx:
         big = ctx.enter_context(tc.tile_pool(name="big", bufs=1))
@@ -46,7 +46,10 @@ def tile_simpleconvolution_t_kernel(tc, x, weight, out):
             x_tiles.append(x_tile)
 
         w_grouped = keep.tile([P, COUT, PACK], BF16, name="w_grouped", align_bytes=64)
-        nc.vector.tensor_copy(out=w_grouped[:], in_=w_raw[:].rearrange("p j o -> p o j"))
+        nc.vector.tensor_copy(
+            out=w_grouped[:].rearrange("p (t m) j -> p t m j", t=O_TILES),
+            in_=w_raw[:].rearrange("p j (m t) -> p t m j", t=O_TILES),
+        )
         w_codes = keep.tile([P, COUT], U32, name="w_codes", align_bytes=64)
         w_scales = keep.tile([P, COUT], U8, name="w_scales", align_bytes=64)
         nc.vector.quantize_mx(
@@ -103,6 +106,9 @@ def tile_simpleconvolution_t_kernel(tc, x, weight, out):
                     )
                     acc_tiles[(g, n, t)] = acc
 
+        def store(b, first, last):
+            nc.sync.dma_start(out=out_rows[b][:, :, first:last], in_=out_tiles[b][:, :, first:last])
+
         def evacuate(g):
             b, q = divmod(g, CHUNKS_PER_IMAGE)
             if q == 0:
@@ -110,15 +116,17 @@ def tile_simpleconvolution_t_kernel(tc, x, weight, out):
             for n in range(CHUNK // N_TILE):
                 first = q * CHUNK + n * N_TILE
                 for t in range(O_TILES):
-                    nc.scalar.copy(
-                        out=out_tiles[b][:, t, first : first + N_TILE], in_=acc_tiles[(g, n, t)][:]
-                    )
-            pieces = 2 if b == BATCH - 1 else 1
-            per_piece = CHUNKS_PER_IMAGE // pieces
-            if (q + 1) % per_piece == 0:
-                px = slice((q + 1 - per_piece) * CHUNK, (q + 1) * CHUNK)
-                for t in range(O_TILES):
-                    nc.sync.dma_start(out=out_rows[b, t][:, px], in_=out_tiles[b][:, t, px])
+                    copy = nc.vector.tensor_copy if (g >= N_CHUNKS - 2 and t == 1) else nc.scalar.copy
+                    copy(out=out_tiles[b][:, t, first : first + N_TILE], in_=acc_tiles[(g, n, t)][:])
+                if g == N_CHUNKS - 1:
+                    store(b, first, first + N_TILE)
+            if b < BATCH - 1:
+                if q == CHUNKS_PER_IMAGE - 1:
+                    store(b, 0, PIXELS)
+            elif q == 1:
+                store(b, 0, 2 * CHUNK)
+            elif q == 2:
+                store(b, 2 * CHUNK, 3 * CHUNK)
 
         for step in range(N_CHUNKS + 2):
             if step < N_CHUNKS:

@@ -26,7 +26,7 @@ def tile_simpleconvolution_t_kernel(tc, x, weight, out):
     nc = tc.nc
     x_rows = x.rearrange("b (p j) h w -> b p j (h w)", j=PACK)
     w_rows = weight.rearrange("(p j) o -> p j o", j=PACK)
-    out_rows = out.rearrange("b (m t) h w -> b m t (h w)", t=O_TILES)
+    out_rows = out.rearrange("b (t o) h w -> b t o (h w)", o=P)
 
     with ExitStack() as ctx:
         big = ctx.enter_context(tc.tile_pool(name="big", bufs=1))
@@ -46,10 +46,7 @@ def tile_simpleconvolution_t_kernel(tc, x, weight, out):
             x_tiles.append(x_tile)
 
         w_grouped = keep.tile([P, COUT, PACK], BF16, name="w_grouped", align_bytes=64)
-        nc.vector.tensor_copy(
-            out=w_grouped[:].rearrange("p (t m) j -> p t m j", t=O_TILES),
-            in_=w_raw[:].rearrange("p j (m t) -> p t m j", t=O_TILES),
-        )
+        nc.vector.tensor_copy(out=w_grouped[:], in_=w_raw[:].rearrange("p j o -> p o j"))
         w_codes = keep.tile([P, COUT], U32, name="w_codes", align_bytes=64)
         w_scales = keep.tile([P, COUT], U8, name="w_scales", align_bytes=64)
         nc.vector.quantize_mx(
@@ -106,9 +103,6 @@ def tile_simpleconvolution_t_kernel(tc, x, weight, out):
                     )
                     acc_tiles[(g, n, t)] = acc
 
-        def store(b, first, last):
-            nc.sync.dma_start(out=out_rows[b][:, :, first:last], in_=out_tiles[b][:, :, first:last])
-
         def evacuate(g):
             b, q = divmod(g, CHUNKS_PER_IMAGE)
             if q == 0:
@@ -116,17 +110,15 @@ def tile_simpleconvolution_t_kernel(tc, x, weight, out):
             for n in range(CHUNK // N_TILE):
                 first = q * CHUNK + n * N_TILE
                 for t in range(O_TILES):
-                    copy = nc.vector.tensor_copy if (g >= N_CHUNKS - 2 and t == 1) else nc.scalar.copy
-                    copy(out=out_tiles[b][:, t, first : first + N_TILE], in_=acc_tiles[(g, n, t)][:])
-                if g == N_CHUNKS - 1:
-                    store(b, first, first + N_TILE)
-            if b < BATCH - 1:
-                if q == CHUNKS_PER_IMAGE - 1:
-                    store(b, 0, PIXELS)
-            elif q == 1:
-                store(b, 0, 2 * CHUNK)
-            elif q == 2:
-                store(b, 2 * CHUNK, 3 * CHUNK)
+                    nc.scalar.copy(
+                        out=out_tiles[b][:, t, first : first + N_TILE], in_=acc_tiles[(g, n, t)][:]
+                    )
+            pieces = 2 if b >= BATCH - 2 else 1
+            per_piece = CHUNKS_PER_IMAGE // pieces
+            if (q + 1) % per_piece == 0:
+                px = slice((q + 1 - per_piece) * CHUNK, (q + 1) * CHUNK)
+                for t in range(O_TILES):
+                    nc.sync.dma_start(out=out_rows[b, t][:, px], in_=out_tiles[b][:, t, px])
 
         for step in range(N_CHUNKS + 2):
             if step < N_CHUNKS:

@@ -12,11 +12,12 @@ BATCH, CIN, COUT, PIXELS = 4, 512, 256, 64 * 64
 P = 128
 PACK = 4
 O_TILES = COUT // P
-CHUNK = 1024
+CHUNK = 512
 CHUNKS_PER_IMAGE = PIXELS // CHUNK
 N_CHUNKS = BATCH * CHUNKS_PER_IMAGE
 N_TILE = 512
-VECTOR_PIXELS = 848
+HALF = CHUNKS_PER_IMAGE // 2
+VECTOR_PIXELS = 424
 RUN = 4
 
 FLOPS = 2 * BATCH * CIN * COUT * PIXELS
@@ -26,12 +27,12 @@ def tile_simpleconvolution_t_kernel(tc, x, weight, out):
     nc = tc.nc
     x_rows = x.rearrange("b (p j) h w -> b p j (h w)", j=PACK)
     w_rows = weight.rearrange("(p j) o -> p j o", j=PACK)
-    out_rows = out.rearrange("b (t o) h w -> b t o (h w)", o=P)
+    out_rows = out.rearrange("b (m t) h w -> b m t (h w)", t=O_TILES)
 
     with ExitStack() as ctx:
         big = ctx.enter_context(tc.tile_pool(name="big", bufs=1))
         keep = ctx.enter_context(tc.tile_pool(name="keep", bufs=1))
-        stage = ctx.enter_context(tc.tile_pool(name="stage", bufs=3))
+        stage = ctx.enter_context(tc.tile_pool(name="stage", bufs=4))
         psum = ctx.enter_context(tc.psum_pool(name="psum", bufs=8))
         ctx.enter_context(tc.manual_schedule())
 
@@ -46,7 +47,10 @@ def tile_simpleconvolution_t_kernel(tc, x, weight, out):
             x_tiles.append(x_tile)
 
         w_grouped = keep.tile([P, COUT, PACK], BF16, name="w_grouped", align_bytes=64)
-        nc.vector.tensor_copy(out=w_grouped[:], in_=w_raw[:].rearrange("p j o -> p o j"))
+        nc.vector.tensor_copy(
+            out=w_grouped[:].rearrange("p (t m) j -> p t m j", t=O_TILES),
+            in_=w_raw[:].rearrange("p j (m t) -> p t m j", t=O_TILES),
+        )
         w_codes = keep.tile([P, COUT], U32, name="w_codes", align_bytes=64)
         w_scales = keep.tile([P, COUT], U8, name="w_scales", align_bytes=64)
         nc.vector.quantize_mx(
@@ -103,6 +107,9 @@ def tile_simpleconvolution_t_kernel(tc, x, weight, out):
                     )
                     acc_tiles[(g, n, t)] = acc
 
+        def store(b, first, last):
+            nc.sync.dma_start(out=out_rows[b][:, :, first:last], in_=out_tiles[b][:, :, first:last])
+
         def evacuate(g):
             b, q = divmod(g, CHUNKS_PER_IMAGE)
             if q == 0:
@@ -110,21 +117,19 @@ def tile_simpleconvolution_t_kernel(tc, x, weight, out):
             for n in range(CHUNK // N_TILE):
                 first = q * CHUNK + n * N_TILE
                 for t in range(O_TILES):
-                    nc.scalar.copy(
-                        out=out_tiles[b][:, t, first : first + N_TILE], in_=acc_tiles[(g, n, t)][:]
-                    )
-            pieces = 2 if b >= BATCH - 2 else 1
-            per_piece = CHUNKS_PER_IMAGE // pieces
-            if (q + 1) % per_piece == 0:
-                px = slice((q + 1 - per_piece) * CHUNK, (q + 1) * CHUNK)
-                for t in range(O_TILES):
-                    nc.sync.dma_start(out=out_rows[b, t][:, px], in_=out_tiles[b][:, t, px])
+                    copy = nc.vector.tensor_copy if (g >= N_CHUNKS - 3 and t == 1) else nc.scalar.copy
+                    copy(out=out_tiles[b][:, t, first : first + N_TILE], in_=acc_tiles[(g, n, t)][:])
+            if b < BATCH - 1:
+                if q == CHUNKS_PER_IMAGE - 1:
+                    store(b, 0, PIXELS)
+            elif (q + 1) % HALF == 0:
+                store(b, (q + 1 - HALF) * CHUNK, (q + 1) * CHUNK)
 
-        for step in range(N_CHUNKS + 2):
+        for step in range(N_CHUNKS + 3):
             if step < N_CHUNKS:
                 regroup(step)
             if 0 <= step - 1 < N_CHUNKS:
                 quantise(step - 1)
                 multiply(step - 1)
-            if step - 2 >= 0:
-                evacuate(step - 2)
+            if step - 3 >= 0:
+                evacuate(step - 3)

@@ -42,7 +42,7 @@ def tile_simpleconvolution_t_kernel(tc, x, weight, out):
         out_slot = {0: "slot3", 1: "slot0", 2: "slot1", 3: "slot2"}
         x_tiles = []
         for b in range(BATCH):
-            x_tile = big.tile([P, PACK, PIXELS], BF16, name="x_tile", tag=x_slot[b])
+            x_tile = big.tile([P, PACK, PIXELS], BF16, name="x_tile", tag=x_slot[b], align_bytes=4096)
             nc.sync.dma_start(out=x_tile[:], in_=x_rows[b])
             x_tiles.append(x_tile)
 
@@ -113,7 +113,7 @@ def tile_simpleconvolution_t_kernel(tc, x, weight, out):
         def evacuate(g):
             b, q = divmod(g, CHUNKS_PER_IMAGE)
             if q == 0:
-                out_tiles[b] = big.tile([P, O_TILES, PIXELS], F32, name="out_tile", tag=out_slot[b])
+                out_tiles[b] = big.tile([P, O_TILES, PIXELS], F32, name="out_tile", tag=out_slot[b], align_bytes=4096)
             for n in range(CHUNK // N_TILE):
                 first = q * CHUNK + n * N_TILE
                 for t in range(O_TILES):

@@ -37,7 +37,7 @@ def tile_simpleconvolution_t_kernel(tc, x, weight, out):
         ctx.enter_context(tc.manual_schedule())
 
         w_raw = keep.tile([P, PACK, COUT], BF16, name="w_raw")
-        nc.sync.dma_start(out=w_raw[:], in_=w_rows)
+        nc.scalar.dma_start(out=w_raw[:], in_=w_rows)
         x_slot = {0: "slot0", 1: "slot1", 2: "slot2", 3: "slot4"}
         out_slot = {0: "slot3", 1: "slot0", 2: "slot1", 3: "slot2"}
         x_tiles = []

@@ -16,8 +16,9 @@ CHUNK = 512
 CHUNKS_PER_IMAGE = PIXELS // CHUNK
 N_CHUNKS = BATCH * CHUNKS_PER_IMAGE
 N_TILE = 512
-HALF = CHUNKS_PER_IMAGE // 2
-VECTOR_PIXELS = 424
+EARLY_CHUNKS = 3
+EARLY_VECTOR_PIXELS = 256
+VECTOR_PIXELS = 416
 RUN = 4
 
 FLOPS = 2 * BATCH * CIN * COUT * PIXELS
@@ -47,17 +48,8 @@ def tile_simpleconvolution_t_kernel(tc, x, weight, out):
             x_tiles.append(x_tile)
 
         w_grouped = keep.tile([P, COUT, PACK], BF16, name="w_grouped", align_bytes=64)
-        nc.vector.tensor_copy(
-            out=w_grouped[:].rearrange("p (t m) j -> p t m j", t=O_TILES),
-            in_=w_raw[:].rearrange("p j (m t) -> p t m j", t=O_TILES),
-        )
         w_codes = keep.tile([P, COUT], U32, name="w_codes", align_bytes=64)
         w_scales = keep.tile([P, COUT], U8, name="w_scales", align_bytes=64)
-        nc.vector.quantize_mx(
-            out=w_codes[:].bitcast(FP8X4),
-            scales=w_scales[:],
-            in_=w_grouped[:].rearrange("p o j -> p (o j)"),
-        )
 
         grouped_tiles = {}
         code_tiles = {}
@@ -67,10 +59,8 @@ def tile_simpleconvolution_t_kernel(tc, x, weight, out):
         def regroup(g):
             b, q = divmod(g, CHUNKS_PER_IMAGE)
             grouped = stage.tile([P, CHUNK, PACK], BF16, name="grouped", align_bytes=64)
-            for copy, lo, hi in (
-                (nc.vector.tensor_copy, 0, VECTOR_PIXELS),
-                (nc.scalar.copy, VECTOR_PIXELS, CHUNK),
-            ):
+            cut = EARLY_VECTOR_PIXELS if g < EARLY_CHUNKS else VECTOR_PIXELS
+            for copy, lo, hi in ((nc.vector.tensor_copy, 0, cut), (nc.scalar.copy, cut, CHUNK)):
                 copy(
                     out=grouped[:, lo:hi, :].rearrange("p (c i) j -> p c j i", i=RUN),
                     in_=x_tiles[b][:, :, q * CHUNK + lo : q * CHUNK + hi].rearrange(
@@ -107,9 +97,6 @@ def tile_simpleconvolution_t_kernel(tc, x, weight, out):
                     )
                     acc_tiles[(g, n, t)] = acc
 
-        def store(b, first, last):
-            nc.sync.dma_start(out=out_rows[b][:, :, first:last], in_=out_tiles[b][:, :, first:last])
-
         def evacuate(g):
             b, q = divmod(g, CHUNKS_PER_IMAGE)
             if q == 0:
@@ -119,15 +106,25 @@ def tile_simpleconvolution_t_kernel(tc, x, weight, out):
                 for t in range(O_TILES):
                     copy = nc.vector.tensor_copy if (g >= N_CHUNKS - 3 and t == 1) else nc.scalar.copy
                     copy(out=out_tiles[b][:, t, first : first + N_TILE], in_=acc_tiles[(g, n, t)][:])
-            if b < BATCH - 1:
-                if q == CHUNKS_PER_IMAGE - 1:
-                    store(b, 0, PIXELS)
-            elif (q + 1) % HALF == 0:
-                store(b, (q + 1 - HALF) * CHUNK, (q + 1) * CHUNK)
+            if q == CHUNKS_PER_IMAGE - 1:
+                nc.sync.dma_start(out=out_rows[b], in_=out_tiles[b][:])
+
+        def prepare_weights():
+            nc.vector.tensor_copy(
+                out=w_grouped[:].rearrange("p (t m) j -> p t m j", t=O_TILES),
+                in_=w_raw[:].rearrange("p j (m t) -> p t m j", t=O_TILES),
+            )
+            nc.vector.quantize_mx(
+                out=w_codes[:].bitcast(FP8X4),
+                scales=w_scales[:],
+                in_=w_grouped[:].rearrange("p o j -> p (o j)"),
+            )
 
         for step in range(N_CHUNKS + 3):
             if step < N_CHUNKS:
                 regroup(step)
+                if step == 0:
+                    prepare_weights()
             if 0 <= step - 1 < N_CHUNKS:
                 quantise(step - 1)
                 multiply(step - 1)

from contextlib import ExitStack

import concourse.mybir as mybir

BF16 = mybir.dt.bfloat16
F32 = mybir.dt.float32
U32 = mybir.dt.uint32
U8 = mybir.dt.uint8
FP8X4 = mybir.dt.float8_e4m3fn_x4

BATCH, CIN, COUT, PIXELS = 4, 512, 256, 64 * 64
P = 128
PACK = 4
O_TILES = COUT // P
CHUNK = 512
CHUNKS_PER_IMAGE = PIXELS // CHUNK
N_CHUNKS = BATCH * CHUNKS_PER_IMAGE
N_TILE = 512
EARLY_CHUNKS = 3
EARLY_VECTOR_PIXELS = 256
VECTOR_PIXELS = 416
RUN = 4

FLOPS = 2 * BATCH * CIN * COUT * PIXELS


def tile_simpleconvolution_t_kernel(tc, x, weight, out):
    nc = tc.nc
    x_rows = x.rearrange("b (p j) h w -> b p j (h w)", j=PACK)
    w_rows = weight.rearrange("(p j) o -> p j o", j=PACK)
    out_rows = out.rearrange("b (m t) h w -> b m t (h w)", t=O_TILES)

    with ExitStack() as ctx:
        big = ctx.enter_context(tc.tile_pool(name="big", bufs=1))
        keep = ctx.enter_context(tc.tile_pool(name="keep", bufs=1))
        stage = ctx.enter_context(tc.tile_pool(name="stage", bufs=4))
        psum = ctx.enter_context(tc.psum_pool(name="psum", bufs=8))
        ctx.enter_context(tc.manual_schedule())

        w_raw = keep.tile([P, PACK, COUT], BF16, name="w_raw")
        nc.scalar.dma_start(out=w_raw[:], in_=w_rows)
        x_slot = {0: "slot0", 1: "slot1", 2: "slot2", 3: "slot4"}
        out_slot = {0: "slot3", 1: "slot0", 2: "slot1", 3: "slot2"}
        x_tiles = []
        for b in range(BATCH):
            x_tile = big.tile([P, PACK, PIXELS], BF16, name="x_tile", tag=x_slot[b], align_bytes=4096)
            nc.sync.dma_start(out=x_tile[:], in_=x_rows[b])
            x_tiles.append(x_tile)

        w_grouped = keep.tile([P, COUT, PACK], BF16, name="w_grouped", align_bytes=64)
        w_codes = keep.tile([P, COUT], U32, name="w_codes", align_bytes=64)
        w_scales = keep.tile([P, COUT], U8, name="w_scales", align_bytes=64)

        grouped_tiles = {}
        code_tiles = {}
        acc_tiles = {}
        out_tiles = {}

        def regroup(g):
            b, q = divmod(g, CHUNKS_PER_IMAGE)
            grouped = stage.tile([P, CHUNK, PACK], BF16, name="grouped", align_bytes=64)
            cut = EARLY_VECTOR_PIXELS if g < EARLY_CHUNKS else VECTOR_PIXELS
            for copy, lo, hi in ((nc.vector.tensor_copy, 0, cut), (nc.scalar.copy, cut, CHUNK)):
                copy(
                    out=grouped[:, lo:hi, :].rearrange("p (c i) j -> p c j i", i=RUN),
                    in_=x_tiles[b][:, :, q * CHUNK + lo : q * CHUNK + hi].rearrange(
                        "p j (c i) -> p c j i", i=RUN
                    ),
                )
            grouped_tiles[g] = grouped

        def quantise(g):
            codes = stage.tile([P, CHUNK], U32, name="codes", align_bytes=64)
            scales = stage.tile([P, CHUNK], U8, name="scales", align_bytes=64)
            nc.vector.quantize_mx(
                out=codes[:].bitcast(FP8X4),
                scales=scales[:],
                in_=grouped_tiles[g][:].rearrange("p c j -> p (c j)"),
            )
            code_tiles[g] = (codes, scales)

        def multiply(g):
            codes, scales = code_tiles[g]
            for n in range(CHUNK // N_TILE):
                cols = slice(n * N_TILE, (n + 1) * N_TILE)
                for t in range(O_TILES):
                    o_cols = slice(t * P, (t + 1) * P)
                    acc = psum.tile([P, N_TILE], F32, name="acc")
                    nc.tensor.matmul_mx(
                        out=acc[:],
                        lhsT=w_codes[:, o_cols].bitcast(FP8X4),
                        lhsT_scale=w_scales[:, o_cols],
                        rhs=codes[:, cols].bitcast(FP8X4),
                        rhs_scale=scales[:, cols],
                        start=True,
                        stop=True,
                    )
                    acc_tiles[(g, n, t)] = acc

        def evacuate(g):
            b, q = divmod(g, CHUNKS_PER_IMAGE)
            if q == 0:
                out_tiles[b] = big.tile([P, O_TILES, PIXELS], F32, name="out_tile", tag=out_slot[b], align_bytes=4096)
            for n in range(CHUNK // N_TILE):
                first = q * CHUNK + n * N_TILE
                for t in range(O_TILES):
                    copy = nc.vector.tensor_copy if (g >= N_CHUNKS - 3 and t == 1) else nc.scalar.copy
                    copy(out=out_tiles[b][:, t, first : first + N_TILE], in_=acc_tiles[(g, n, t)][:])
            if q == CHUNKS_PER_IMAGE - 1:
                nc.sync.dma_start(out=out_rows[b], in_=out_tiles[b][:])

        def prepare_weights():
            nc.vector.tensor_copy(
                out=w_grouped[:].rearrange("p (t m) j -> p t m j", t=O_TILES),
                in_=w_raw[:].rearrange("p j (m t) -> p t m j", t=O_TILES),
            )
            nc.vector.quantize_mx(
                out=w_codes[:].bitcast(FP8X4),
                scales=w_scales[:],
                in_=w_grouped[:].rearrange("p o j -> p (o j)"),
            )

        for step in range(N_CHUNKS + 3):
            if step < N_CHUNKS:
                regroup(step)
                if step == 0:
                    prepare_weights()
            if 0 <= step - 1 < N_CHUNKS:
                quantise(step - 1)
                multiply(step - 1)
            if step - 3 >= 0:
                evacuate(step - 3)
